import numpy as np
import ml_dtypes


def mxq(x, axis, fmt="e4m3"):
    dtype, down = {"e4m3": (ml_dtypes.float8_e4m3fn, 7), "e5m2": (ml_dtypes.float8_e5m2, 14)}[fmt]
    v = np.moveaxis(np.asarray(x, np.float32).astype(ml_dtypes.bfloat16).astype(np.float64), axis, -1)
    blocks = v.reshape(v.shape[:-1] + (-1, 32))
    amax = np.abs(blocks).max(-1, keepdims=True)
    byte = np.maximum(np.where(amax > 0, np.frexp(amax)[1] - 1 + 127, 0) - down, 1)
    scale = np.exp2(byte - 127.0)
    codes = (blocks / scale).astype(np.float32).astype(dtype).astype(np.float64)
    return np.moveaxis((codes * scale).reshape(v.shape), -1, axis)


WIDE = False


def mx_kscale(k):
    if not WIDE:
        return np.ones(k)
    levels = np.array([10, -10, 5, -5, 0])
    if k % 512:
        return np.exp2(np.random.permutation(np.resize(levels, k // 32))).repeat(32)
    a = np.empty((k // 512, 16))
    for p in range(k // 512):
        a[p, :8] = np.random.permutation(np.resize(levels, 8))
        for g in range(8):
            far = levels[np.abs(levels - a[p, g]) >= 10]
            a[p, g + 8] = far[np.random.randint(len(far))]
    return np.exp2(a.ravel()).repeat(32)


BF16 = ml_dtypes.bfloat16


def bf(x):
    return np.asarray(x, np.float32).astype(BF16)


def f64(x):
    return np.asarray(x).astype(np.float64)


B, N, DIM, H, KD, D = 4, 256, 1024, 12, 64, 128
DH = H * D
EPS = 1e-5


def hard_swish(v):
    return v * (np.minimum(np.maximum(v + 3.0, 0.0), 6.0) / 6.0)


def setup_inputs():
    t = mx_kscale(DH)
    c = 2.0 ** (-8.0 * np.random.random(DIM))
    return {"h_attn": bf(1.5 * np.random.standard_normal((B, N, DH)) * t),
            "proj_w": bf(np.random.standard_normal((DIM, DH)) * c[:, None] / np.sqrt(DH) / t),
            "proj_g": bf(1.0 + 0.1 * np.random.standard_normal(DIM)),
            "proj_b": bf(0.1 * np.random.standard_normal(DIM))}


def bn(y, g, b):
    m = y.mean(axis=(0, 1))
    v = ((y - m) ** 2).mean(axis=(0, 1))
    return (y - m) * (g / np.sqrt(v + EPS)) + b


def reference(h_attn, proj_w, proj_g, proj_b):
    h = hard_swish(f64(h_attn))
    y = mxq(h, 2, "e4m3") @ mxq(f64(proj_w), 1, "e4m3").T
    return bn(y, f64(proj_g), f64(proj_b))

@@ -1,0 +1,280 @@
+import concourse.mybir as mybir
+from concourse.masks import make_identity
+
+F32 = mybir.dt.float32
+BF16 = mybir.dt.bfloat16
+U32 = mybir.dt.uint32
+U8 = mybir.dt.uint8
+FP8X4 = mybir.dt.float8_e4m3fn_x4
+ACT = mybir.ActivationFunctionType
+ALU = mybir.AluOpType
+
+P = 128
+ROWS = 1024
+FEATS = 1024
+K = 1536
+K_PASS = 512
+WORDS = K_PASS // 2
+PASSES = K // K_PASS
+BANK = 512
+HALVES = 2
+FEAT_TILES = FEATS // P
+JOB = 256
+JOBS = BANK // JOB
+H_BANKS = 4
+IN_FLIGHT = 3
+EPS = 1e-5
+
+FLOPS = 2 * ROWS * FEATS * K
+
+
+def tile_attention_pb_kernel(tc, h_attn, proj_w, proj_g, proj_b, out):
+    nc = tc.nc
+    h_flat = h_attn.flatten_outer_dims()
+    out_flat = out.flatten_outer_dims()
+    steps = [(g, half) for g in range(PASSES) for half in range(HALVES)]
+
+    with tc.tile_pool(name="keep", bufs=1) as keep, tc.tile_pool(name="work", bufs=3) as work, tc.tile_pool(
+        name="small", bufs=4
+    ) as small, tc.psum_pool(name="psum", bufs=1) as psum, tc.manual_schedule():
+        h_raw = {}
+        w_raw = {}
+
+        def load_h(g, half, j):
+            h_raw[(g, half, j)] = keep.tile([P, JOB // P, K_PASS], BF16, name="h_raw_%d_%d_%d" % (g, half, j))
+            rows = h_flat[half * BANK : (half + 1) * BANK, g * K_PASS : (g + 1) * K_PASS]
+            nc.sync.dma_start(
+                out=h_raw[(g, half, j)][:], in_=rows.rearrange("(i p j) k -> j p i k", p=P, j=JOBS)[j]
+            )
+
+        def load_w(g, half, j):
+            w_raw[(g, half, j)] = keep.tile([P, JOB // P, K_PASS], BF16, name="w_raw_%d_%d_%d" % (g, half, j))
+            feat0 = half * BANK + j * JOB
+            nc.sync.dma_start(
+                out=w_raw[(g, half, j)][:],
+                in_=proj_w[feat0 : feat0 + JOB, g * K_PASS : (g + 1) * K_PASS].rearrange("(i p) k -> p i k", p=P),
+            )
+
+        gb_rows = keep.tile([P, P], BF16)
+        nc.vector.memset(gb_rows[:], 0.0)
+        nc.scalar.dma_start(out=gb_rows[0:FEAT_TILES, :], in_=proj_g.rearrange("(f p) -> f p", p=P))
+        nc.scalar.dma_start(out=gb_rows[FEAT_TILES : 2 * FEAT_TILES, :], in_=proj_b.rearrange("(f p) -> f p", p=P))
+
+        for g, half in steps:
+            load_h(g, half, 0)
+            load_w(g, 0, half)
+            load_h(g, half, 1)
+        for g in range(PASSES):
+            for j in range(JOBS):
+                load_w(g, 1, j)
+
+        ident = keep.tile([P, P], F32)
+        make_identity(nc, ident[:])
+        minus_half = keep.tile([P, 1], F32)
+        nc.gpsimd.memset(minus_half[:], -0.5)
+
+        one = keep.tile([P, 1], F32)
+        nc.vector.memset(one[:], 1.0)
+        warm = keep.tile([P, 1], F32)
+        nc.scalar.activation(out=warm[:], in_=one[:], func=ACT.Relu)
+
+        gb_f32 = keep.tile([P, P], F32)
+        nc.vector.tensor_copy(out=gb_f32[:], in_=gb_rows[:])
+
+        h_codes = {}
+        h_scales = {}
+        w_codes = {}
+        w_scales = {}
+        for g, half in steps:
+            h_codes[(g, half)] = keep.tile([P, BANK], U32, align_bytes=64, name="h_codes_%d_%d" % (g, half))
+            h_scales[(g, half)] = keep.tile([P, BANK], U8, align_bytes=64, name="h_scales_%d_%d" % (g, half))
+            w_codes[(g, half)] = keep.tile([P, BANK], U32, align_bytes=64, name="w_codes_%d_%d" % (g, half))
+            w_scales[(g, half)] = keep.tile([P, BANK], U8, align_bytes=64, name="w_scales_%d_%d" % (g, half))
+
+        def hard_swish_job(g, half, j, bank_tag, grouped):
+            h_bank = psum.tile([P, 2 * JOB], F32, tag=bank_tag)
+            for i in range(JOB // P):
+                words = h_raw[(g, half, j)][:, i, :].bitcast(F32)
+                part = h_bank[:, i * 2 * P : (i + 1) * 2 * P].rearrange("p (m u par) -> p u m par", u=2, par=2)
+                for u in range(2):
+                    nc.tensor.transpose(part[:, u, :, :], words[:, u:WORDS:2], ident[:])
+            v = h_bank[:].bitcast(BF16).rearrange("p (y par e) -> p par y e", par=2, e=2)
+            ramp = work.tile([P, 2, JOB, 2], F32, tag="ramp")
+            nc.scalar.activation(out=ramp[:], in_=v, func=ACT.Relu, bias=0.5, scale=1.0 / 6.0)
+            for par in range(2):
+                col0 = (2 * j + par) * 2 * JOB
+                nc.vector.scalar_tensor_tensor(
+                    out=grouped[:, col0 : col0 + 2 * JOB].rearrange("p (y e) -> p y e", e=2),
+                    in0=ramp[:, par, :, :],
+                    scalar=1.0,
+                    in1=v[:, par, :, :],
+                    op0=ALU.min,
+                    op1=ALU.mult,
+                )
+
+        def regroup_w_job(g, half, j, grouped):
+            w_bank = psum.tile([P, 2, JOB], F32, tag="bank%d" % (2 * IN_FLIGHT + j))
+            for i in range(JOB // P):
+                words = w_raw[(g, half, j)][:, i, :].bitcast(F32)
+                for u in range(2):
+                    nc.tensor.transpose(w_bank[:, u, i * P : (i + 1) * P], words[:, u:WORDS:2], ident[:])
+            nc.scalar.copy(
+                out=grouped.bitcast(F32).rearrange("p (c u) -> p c u", u=2),
+                in_=w_bank[:].rearrange("p u c -> p c u"),
+            )
+
+        h_grouped = {}
+
+        def quantise_h(s):
+            nc.vector.quantize_mx(
+                out=h_codes[steps[s]][:].bitcast(FP8X4), scales=h_scales[steps[s]][:], in_=h_grouped[s][:]
+            )
+
+        for s, (g, half) in enumerate(steps):
+            h_grouped[s] = work.tile([P, 4 * BANK], BF16, align_bytes=64, tag="h_grouped", name="h_grouped_%d" % s)
+            hard_swish_job(g, half, 0, "bank%d" % (2 + (JOBS * s) % H_BANKS), h_grouped[s])
+            if s > 0:
+                quantise_h(s - 1)
+            w_grouped = work.tile([P, 4 * JOB], BF16, align_bytes=64, tag="w_grouped")
+            regroup_w_job(g, 0, half, w_grouped[:])
+            feats = slice(half * JOB, (half + 1) * JOB)
+            nc.vector.quantize_mx(
+                out=w_codes[(g, 0)][:, feats].bitcast(FP8X4), scales=w_scales[(g, 0)][:, feats], in_=w_grouped[:]
+            )
+            hard_swish_job(g, half, 1, "bank%d" % (2 + (JOBS * s + 1) % H_BANKS), h_grouped[s])
+            if s == 0:
+                gb_bank = psum.tile([P, BANK], F32, tag="bank0")
+                nc.tensor.transpose(gb_bank[:, 0:P], gb_f32[:], ident[:])
+                gain_pm = keep.tile([P, FEAT_TILES, 2], F32)
+                nc.scalar.copy(out=gain_pm[:, :, 0], in_=gb_bank[:, 0:FEAT_TILES])
+                nc.scalar.mul(out=gain_pm[:, :, 1], in_=gb_bank[:, 0:FEAT_TILES], mul=-1.0)
+                beta = keep.tile([P, FEAT_TILES], F32)
+                nc.scalar.copy(out=beta[:], in_=gb_bank[:, FEAT_TILES : 2 * FEAT_TILES])
+        quantise_h(len(steps) - 1)
+
+        late_w_grouped = {}
+
+        def regroup_late_w(g):
+            late_w_grouped[g] = work.tile(
+                [P, 4 * BANK], BF16, align_bytes=64, tag="late_w_grouped", name="late_w_grouped_%d" % g
+            )
+            for j in range(JOBS):
+                regroup_w_job(g, 1, j, late_w_grouped[g][:, j * 4 * JOB : (j + 1) * 4 * JOB])
+
+        y = {}
+
+        def products(f, half, passes):
+            feats = slice((f % (BANK // P)) * P, (f % (BANK // P) + 1) * P)
+            if passes[0] == 0:
+                y[(f, half)] = psum.tile(
+                    [P, BANK], F32, tag="bank%d" % (2 * (f % IN_FLIGHT) + half), name="y_%d_%d" % (f, half)
+                )
+            for g in passes:
+                nc.tensor.matmul_mx(
+                    out=y[(f, half)][:],
+                    lhsT=w_codes[(g, f // (BANK // P))][:, feats].bitcast(FP8X4),
+                    lhsT_scale=w_scales[(g, f // (BANK // P))][:, feats],
+                    rhs=h_codes[(g, half)][:].bitcast(FP8X4),
+                    rhs_scale=h_scales[(g, half)][:],
+                    start=(g == 0),
+                    stop=(g == PASSES - 1),
+                )
+
+        scale_pm = {}
+        shift = {}
+
+        def statistics(f):
+            stats = small.tile([P, HALVES, 6], F32, tag="stats")
+            for half in range(HALVES):
+                nc.vector.bn_stats(out=stats[:, half, :], in_=y[(f, half)][:])
+            mean_var = small.tile([P, 2], F32, tag="mean_var")
+            nc.vector.bn_aggr(out=mean_var[:], in_=stats[:].rearrange("p a s -> p (a s)"))
+            var_eps = small.tile([P, 1], F32, tag="var_eps")
+            nc.gpsimd.tensor_scalar(
+                out=var_eps[:], in0=mean_var[:, 1:2], scalar1=EPS, scalar2=1.0, op0=ALU.add, op1=ALU.mult
+            )
+            rstd = small.tile([P, 1], F32, tag="rstd")
+            nc.gpsimd.tensor_tensor(out=rstd[:], in0=var_eps[:], in1=minus_half[:], op=ALU.pow)
+            scale_pm[f] = small.tile([P, 2], F32, tag="scale_pm", name="scale_pm_%d" % f)
+            nc.gpsimd.tensor_scalar(
+                out=scale_pm[f][:], in0=gain_pm[:, f, :], scalar1=rstd[:], scalar2=1.0, op0=ALU.mult, op1=ALU.mult
+            )
+            shift[f] = small.tile([P, 1], F32, tag="shift", name="shift_%d" % f)
+            nc.gpsimd.tensor_scalar(
+                out=shift[f][:],
+                in0=mean_var[:, 0:1],
+                scalar1=scale_pm[f][:, 1:2],
+                scalar2=beta[:, f : f + 1],
+                op0=ALU.mult,
+                op1=ALU.add,
+            )
+
+        z = {}
+
+        def norm(f):
+            for half in range(HALVES):
+                z[(f, half)] = work.tile([P, BANK], F32, tag="z%d" % half, name="z_%d_%d" % (f, half))
+                nc.scalar.activation(
+                    out=z[(f, half)][:],
+                    in_=y[(f, half)][:],
+                    func=ACT.Identity,
+                    bias=shift[f][:],
+                    scale=scale_pm[f][:, 0:1],
+                )
+
+        zt = {}
+
+        def transposes_back(f):
+            for half in range(HALVES):
+                zt[(f, half)] = psum.tile(
+                    [P, BANK // P, P], F32, tag="bank%d" % (2 * IN_FLIGHT + half), name="zt_%d_%d" % (f, half)
+                )
+                for j in range(JOBS):
+                    for par in range(2):
+                        i = 2 * j + par
+                        nc.tensor.transpose(zt[(f, half)][:, 2 * par + j, :], z[(f, half)][:, i * P : (i + 1) * P], ident[:])
+
+        def store(f):
+            for half in range(HALVES):
+                o = work.tile([P, BANK // P, P], F32, tag="o%d" % half)
+                if half == 0:
+                    nc.vector.tensor_copy(out=o[:], in_=zt[(f, half)][:])
+                else:
+                    nc.scalar.copy(out=o[:], in_=zt[(f, half)][:])
+                nc.sync.dma_start(
+                    out=out_flat[half * BANK : (half + 1) * BANK, f * P : (f + 1) * P].rearrange(
+                        "(p m) c -> p m c", p=P
+                    ),
+                    in_=o[:],
+                )
+
+        for f in range(IN_FLIGHT - 1):
+            for half in range(HALVES):
+                products(f, half, [0, 1])
+        regroup_late_w(0)
+        for f in range(IN_FLIGHT - 1):
+            products(f, 0, [2])
+        regroup_late_w(1)
+        for f in range(IN_FLIGHT - 1):
+            products(f, 1, [2])
+        regroup_late_w(2)
+        for half in range(HALVES):
+            products(IN_FLIGHT - 1, half, list(range(PASSES)))
+
+        for f in range(IN_FLIGHT - 1):
+            statistics(f)
+            norm(f)
+        for g in range(PASSES):
+            nc.vector.quantize_mx(
+                out=w_codes[(g, 1)][:].bitcast(FP8X4), scales=w_scales[(g, 1)][:], in_=late_w_grouped[g][:]
+            )
+        for f in range(FEAT_TILES):
+            if f + IN_FLIGHT - 1 < FEAT_TILES:
+                statistics(f + IN_FLIGHT - 1)
+            transposes_back(f)
+            if f + IN_FLIGHT < FEAT_TILES:
+                for half in range(HALVES):
+                    products(f + IN_FLIGHT, half, list(range(PASSES)))
+            store(f)
+            if f + IN_FLIGHT - 1 < FEAT_TILES:
+                norm(f + IN_FLIGHT - 1)

@@ -21,9 +21,19 @@ HALVES = 2
 FEAT_TILES = FEATS // P
 JOB = 256
 JOBS = BANK // JOB
-H_BANKS = 4
-IN_FLIGHT = 3
+STEPS = HALVES * PASSES
+H_JOBS = STEPS * JOBS
+IN_FLIGHT = 4
+LEAD = 2
 EPS = 1e-5
+W_BESIDE = [1, 2, 1, 2, 1, 2, 1, 2, 0, 0, 0, 0]
+W_ON_VECTOR = (2, 5)
+PRODUCTS_AT = {7: [0], 8: [1, 2], 9: [3], 10: [4], 11: [5]}
+KEEP_AT = {8: [0], 9: [1, 2], 10: [3], 11: [4]}
+STATS_AT = {}
+X_ON_VECTOR = (1, 4, 7)
+Z_ENGINE = "gpsimd"
+SPLIT_FIRST = True
 
 FLOPS = 2 * ROWS * FEATS * K
 
@@ -32,7 +42,9 @@ def tile_attention_pb_kernel(tc, h_attn, proj_w, proj_g, proj_b, out):
     nc = tc.nc
     h_flat = h_attn.flatten_outer_dims()
     out_flat = out.flatten_outer_dims()
-    steps = [(g, half) for g in range(PASSES) for half in range(HALVES)]
+    h_jobs = [(half, g, j) for half in range(HALVES) for g in range(PASSES) for j in range(JOBS)]
+    w_jobs = [(fh, g, j) for fh in range(HALVES) for g in range(PASSES) for j in range(JOBS)]
+    w_slots = [w_jobs[sum(W_BESIDE[:n]) : sum(W_BESIDE[: n + 1])] for n in range(H_JOBS)]
 
     with tc.tile_pool(name="keep", bufs=1) as keep, tc.tile_pool(name="work", bufs=3) as work, tc.tile_pool(
         name="small", bufs=4
@@ -40,18 +52,18 @@ def tile_attention_pb_kernel(tc, h_attn, proj_w, proj_g, proj_b, out):
         h_raw = {}
         w_raw = {}
 
-        def load_h(g, half, j):
-            h_raw[(g, half, j)] = keep.tile([P, JOB // P, K_PASS], BF16, name="h_raw_%d_%d_%d" % (g, half, j))
+        def load_h(half, g, j):
+            h_raw[(half, g, j)] = keep.tile([P, JOB // P, K_PASS], BF16, name="h_raw_%d_%d_%d" % (half, g, j))
             rows = h_flat[half * BANK : (half + 1) * BANK, g * K_PASS : (g + 1) * K_PASS]
             nc.sync.dma_start(
-                out=h_raw[(g, half, j)][:], in_=rows.rearrange("(i p j) k -> j p i k", p=P, j=JOBS)[j]
+                out=h_raw[(half, g, j)][:], in_=rows.rearrange("(i p j) k -> j p i k", p=P, j=JOBS)[j]
             )
 
-        def load_w(g, half, j):
-            w_raw[(g, half, j)] = keep.tile([P, JOB // P, K_PASS], BF16, name="w_raw_%d_%d_%d" % (g, half, j))
-            feat0 = half * BANK + j * JOB
+        def load_w(fh, g, j):
+            w_raw[(fh, g, j)] = keep.tile([P, JOB // P, K_PASS], BF16, name="w_raw_%d_%d_%d" % (fh, g, j))
+            feat0 = fh * BANK + j * JOB
             nc.sync.dma_start(
-                out=w_raw[(g, half, j)][:],
+                out=w_raw[(fh, g, j)][:],
                 in_=proj_w[feat0 : feat0 + JOB, g * K_PASS : (g + 1) * K_PASS].rearrange("(i p) k -> p i k", p=P),
             )
 
@@ -60,151 +72,161 @@ def tile_attention_pb_kernel(tc, h_attn, proj_w, proj_g, proj_b, out):
         nc.scalar.dma_start(out=gb_rows[0:FEAT_TILES, :], in_=proj_g.rearrange("(f p) -> f p", p=P))
         nc.scalar.dma_start(out=gb_rows[FEAT_TILES : 2 * FEAT_TILES, :], in_=proj_b.rearrange("(f p) -> f p", p=P))
 
-        for g, half in steps:
-            load_h(g, half, 0)
-            load_w(g, 0, half)
-            load_h(g, half, 1)
-        for g in range(PASSES):
-            for j in range(JOBS):
-                load_w(g, 1, j)
+        for n in range(H_JOBS):
+            load_h(*h_jobs[n])
+            for w_job in w_slots[n]:
+                load_w(*w_job)
 
         ident = keep.tile([P, P], F32)
         make_identity(nc, ident[:])
-        minus_half = keep.tile([P, 1], F32)
-        nc.gpsimd.memset(minus_half[:], -0.5)
 
         one = keep.tile([P, 1], F32)
         nc.vector.memset(one[:], 1.0)
         warm = keep.tile([P, 1], F32)
-        nc.scalar.activation(out=warm[:], in_=one[:], func=ACT.Relu)
+        nc.scalar.activation(out=warm[:], in_=one[:], func=ACT.Abs_reciprocal_sqrt)
 
         gb_f32 = keep.tile([P, P], F32)
-        nc.vector.tensor_copy(out=gb_f32[:], in_=gb_rows[:])
+        nc.gpsimd.tensor_copy(out=gb_f32[:], in_=gb_rows[:])
 
         h_codes = {}
         h_scales = {}
         w_codes = {}
         w_scales = {}
-        for g, half in steps:
-            h_codes[(g, half)] = keep.tile([P, BANK], U32, align_bytes=64, name="h_codes_%d_%d" % (g, half))
-            h_scales[(g, half)] = keep.tile([P, BANK], U8, align_bytes=64, name="h_scales_%d_%d" % (g, half))
-            w_codes[(g, half)] = keep.tile([P, BANK], U32, align_bytes=64, name="w_codes_%d_%d" % (g, half))
-            w_scales[(g, half)] = keep.tile([P, BANK], U8, align_bytes=64, name="w_scales_%d_%d" % (g, half))
+        for half in range(HALVES):
+            for g in range(PASSES):
+                key = (half, g)
+                h_codes[key] = keep.tile([P, BANK], U32, align_bytes=64, name="h_codes_%d_%d" % key)
+                h_scales[key] = keep.tile([P, BANK], U8, align_bytes=64, name="h_scales_%d_%d" % key)
+                w_codes[key] = keep.tile([P, BANK], U32, align_bytes=64, name="w_codes_%d_%d" % key)
+                w_scales[key] = keep.tile([P, BANK], U8, align_bytes=64, name="w_scales_%d_%d" % key)
 
-        def hard_swish_job(g, half, j, bank_tag, grouped):
-            h_bank = psum.tile([P, 2 * JOB], F32, tag=bank_tag)
-            for i in range(JOB // P):
-                words = h_raw[(g, half, j)][:, i, :].bitcast(F32)
-                part = h_bank[:, i * 2 * P : (i + 1) * 2 * P].rearrange("p (m u par) -> p u m par", u=2, par=2)
-                for u in range(2):
-                    nc.tensor.transpose(part[:, u, :, :], words[:, u:WORDS:2], ident[:])
-            v = h_bank[:].bitcast(BF16).rearrange("p (y par e) -> p par y e", par=2, e=2)
-            ramp = work.tile([P, 2, JOB, 2], F32, tag="ramp")
-            nc.scalar.activation(out=ramp[:], in_=v, func=ACT.Relu, bias=0.5, scale=1.0 / 6.0)
-            for par in range(2):
-                col0 = (2 * j + par) * 2 * JOB
-                nc.vector.scalar_tensor_tensor(
-                    out=grouped[:, col0 : col0 + 2 * JOB].rearrange("p (y e) -> p y e", e=2),
-                    in0=ramp[:, par, :, :],
-                    scalar=1.0,
-                    in1=v[:, par, :, :],
-                    op0=ALU.min,
-                    op1=ALU.mult,
+        h_banks = {}
+
+        def transpose_h(n):
+            pieces = JOB // P if SPLIT_FIRST and n == 0 else 1
+            h_banks[n] = []
+            for piece in range(pieces):
+                bank = psum.tile(
+                    [P, 2 * JOB // pieces], F32, tag="bank%d" % ((n + 3 * piece) % 4), name="h_bank_%d_%d" % (n, piece)
                 )
-
-        def regroup_w_job(g, half, j, grouped):
-            w_bank = psum.tile([P, 2, JOB], F32, tag="bank%d" % (2 * IN_FLIGHT + j))
-            for i in range(JOB // P):
-                words = w_raw[(g, half, j)][:, i, :].bitcast(F32)
-                for u in range(2):
-                    nc.tensor.transpose(w_bank[:, u, i * P : (i + 1) * P], words[:, u:WORDS:2], ident[:])
-            nc.scalar.copy(
-                out=grouped.bitcast(F32).rearrange("p (c u) -> p c u", u=2),
-                in_=w_bank[:].rearrange("p u c -> p c u"),
-            )
+                h_banks[n].append(bank)
+                for i in range(JOB // P // pieces):
+                    words = h_raw[h_jobs[n]][:, piece + i, :].bitcast(F32)
+                    part = bank[:, i * 2 * P : (i + 1) * 2 * P].rearrange("p (m u par) -> p u m par", u=2, par=2)
+                    for u in range(2):
+                        nc.tensor.transpose(part[:, u, :, :], words[:, u:WORDS:2], ident[:])
 
         h_grouped = {}
 
-        def quantise_h(s):
+        def hard_swish(n):
+            half, g, j = h_jobs[n]
+            if j == 0:
+                h_grouped[(half, g)] = work.tile(
+                    [P, 4 * BANK], BF16, align_bytes=64, tag="h_grouped", name="h_grouped_%d_%d" % (half, g)
+                )
+            pieces = len(h_banks[n])
+            for piece in range(pieces):
+                ramp = work.tile([P, 2, JOB // pieces, 2], F32, tag="ramp")
+                v = h_banks[n][piece][:].bitcast(BF16).rearrange("p (y par e) -> p par y e", par=2, e=2)
+                ys = slice(piece * JOB // pieces, (piece + 1) * JOB // pieces)
+                nc.scalar.activation(out=ramp[:], in_=v, func=ACT.Relu, bias=0.5, scale=1.0 / 6.0)
+                for par in range(2):
+                    cols = h_grouped[(half, g)][:, (2 * j + par) * 2 * JOB : (2 * j + par + 1) * 2 * JOB]
+                    nc.vector.scalar_tensor_tensor(
+                        out=cols.rearrange("p (y e) -> p y e", e=2)[:, ys, :],
+                        in0=ramp[:, par, :, :],
+                        scalar=1.0,
+                        in1=v[:, par, :, :],
+                        op0=ALU.min,
+                        op1=ALU.mult,
+                    )
+
+        def quantise_h(half, g):
             nc.vector.quantize_mx(
-                out=h_codes[steps[s]][:].bitcast(FP8X4), scales=h_scales[steps[s]][:], in_=h_grouped[s][:]
+                out=h_codes[(half, g)][:].bitcast(FP8X4), scales=h_scales[(half, g)][:], in_=h_grouped[(half, g)][:]
             )
 
-        for s, (g, half) in enumerate(steps):
-            h_grouped[s] = work.tile([P, 4 * BANK], BF16, align_bytes=64, tag="h_grouped", name="h_grouped_%d" % s)
-            hard_swish_job(g, half, 0, "bank%d" % (2 + (JOBS * s) % H_BANKS), h_grouped[s])
-            if s > 0:
-                quantise_h(s - 1)
-            w_grouped = work.tile([P, 4 * JOB], BF16, align_bytes=64, tag="w_grouped")
-            regroup_w_job(g, 0, half, w_grouped[:])
-            feats = slice(half * JOB, (half + 1) * JOB)
+        w_grouped = {}
+
+        def regroup_w(fh, g, j):
+            if j == 0:
+                w_grouped[(fh, g)] = work.tile(
+                    [P, 4 * BANK], BF16, align_bytes=64, tag="w_grouped", name="w_grouped_%d_%d" % (fh, g)
+                )
+            w_bank = psum.tile([P, 2, JOB], F32, tag="bank%d" % (4 + j))
+            for i in range(JOB // P):
+                words = w_raw[(fh, g, j)][:, i, :].bitcast(F32)
+                for u in range(2):
+                    nc.tensor.transpose(w_bank[:, u, i * P : (i + 1) * P], words[:, u:WORDS:2], ident[:])
+            (nc.vector.tensor_copy if w_jobs.index((fh, g, j)) in W_ON_VECTOR else nc.scalar.copy)(
+                out=w_grouped[(fh, g)][:, j * 4 * JOB : (j + 1) * 4 * JOB].bitcast(F32).rearrange("p (c u) -> p c u", u=2),
+                in_=w_bank[:].rearrange("p u c -> p c u"),
+            )
+
+        def quantise_w(fh, g):
             nc.vector.quantize_mx(
-                out=w_codes[(g, 0)][:, feats].bitcast(FP8X4), scales=w_scales[(g, 0)][:, feats], in_=w_grouped[:]
+                out=w_codes[(fh, g)][:].bitcast(FP8X4), scales=w_scales[(fh, g)][:], in_=w_grouped[(fh, g)][:]
             )
-            hard_swish_job(g, half, 1, "bank%d" % (2 + (JOBS * s + 1) % H_BANKS), h_grouped[s])
-            if s == 0:
-                gb_bank = psum.tile([P, BANK], F32, tag="bank0")
-                nc.tensor.transpose(gb_bank[:, 0:P], gb_f32[:], ident[:])
-                gain_pm = keep.tile([P, FEAT_TILES, 2], F32)
-                nc.scalar.copy(out=gain_pm[:, :, 0], in_=gb_bank[:, 0:FEAT_TILES])
-                nc.scalar.mul(out=gain_pm[:, :, 1], in_=gb_bank[:, 0:FEAT_TILES], mul=-1.0)
-                beta = keep.tile([P, FEAT_TILES], F32)
-                nc.scalar.copy(out=beta[:], in_=gb_bank[:, FEAT_TILES : 2 * FEAT_TILES])
-        quantise_h(len(steps) - 1)
-
-        late_w_grouped = {}
-
-        def regroup_late_w(g):
-            late_w_grouped[g] = work.tile(
-                [P, 4 * BANK], BF16, align_bytes=64, tag="late_w_grouped", name="late_w_grouped_%d" % g
-            )
-            for j in range(JOBS):
-                regroup_w_job(g, 1, j, late_w_grouped[g][:, j * 4 * JOB : (j + 1) * 4 * JOB])
 
         y = {}
 
-        def products(f, half, passes):
+        def products(f, half, passes, bank):
+            fh = f // (BANK // P)
             feats = slice((f % (BANK // P)) * P, (f % (BANK // P) + 1) * P)
             if passes[0] == 0:
-                y[(f, half)] = psum.tile(
-                    [P, BANK], F32, tag="bank%d" % (2 * (f % IN_FLIGHT) + half), name="y_%d_%d" % (f, half)
-                )
+                y[(f, half)] = psum.tile([P, BANK], F32, tag="bank%d" % bank, name="y_%d_%d" % (f, half))
             for g in passes:
                 nc.tensor.matmul_mx(
                     out=y[(f, half)][:],
-                    lhsT=w_codes[(g, f // (BANK // P))][:, feats].bitcast(FP8X4),
-                    lhsT_scale=w_scales[(g, f // (BANK // P))][:, feats],
-                    rhs=h_codes[(g, half)][:].bitcast(FP8X4),
-                    rhs_scale=h_scales[(g, half)][:],
+                    lhsT=w_codes[(fh, g)][:, feats].bitcast(FP8X4),
+                    lhsT_scale=w_scales[(fh, g)][:, feats],
+                    rhs=h_codes[(half, g)][:].bitcast(FP8X4),
+                    rhs_scale=h_scales[(half, g)][:],
                     start=(g == 0),
                     stop=(g == PASSES - 1),
                 )
 
-        scale_pm = {}
+        y_kept = {}
+        stats = {}
+
+        def keep_early(f):
+            y_kept[f] = keep.tile([P, BANK], F32, name="y_kept_%d" % f)
+            nc.scalar.copy(out=y_kept[f][:], in_=y[(f, 0)][:])
+
+        def early_statistics(f):
+            stats[f] = keep.tile([P, HALVES, 6], F32, name="stats_%d" % f)
+            nc.vector.bn_stats(out=stats[f][:, 0, :], in_=y_kept[f][:])
+
+        scale = {}
         shift = {}
 
-        def statistics(f):
-            stats = small.tile([P, HALVES, 6], F32, tag="stats")
-            for half in range(HALVES):
-                nc.vector.bn_stats(out=stats[:, half, :], in_=y[(f, half)][:])
-            mean_var = small.tile([P, 2], F32, tag="mean_var")
-            nc.vector.bn_aggr(out=mean_var[:], in_=stats[:].rearrange("p a s -> p (a s)"))
-            var_eps = small.tile([P, 1], F32, tag="var_eps")
-            nc.gpsimd.tensor_scalar(
-                out=var_eps[:], in0=mean_var[:, 1:2], scalar1=EPS, scalar2=1.0, op0=ALU.add, op1=ALU.mult
+        def late_stats(f):
+            nc.vector.bn_stats(out=stats[f][:, 1, :], in_=y[(f, 1)][:])
+
+        mean_var = {}
+        rstd = {}
+
+        def aggregate(f):
+            mean_var[f] = small.tile([P, 2], F32, tag="mean_var", name="mean_var_%d" % f)
+            nc.vector.bn_aggr(out=mean_var[f][:], in_=stats[f][:].rearrange("p a s -> p (a s)"))
+            rstd[f] = small.tile([P, 1], F32, tag="rstd", name="rstd_%d" % f)
+            nc.scalar.activation(
+                out=rstd[f][:], in_=mean_var[f][:, 1:2], func=ACT.Abs_reciprocal_sqrt, bias=EPS, scale=1.0
             )
-            rstd = small.tile([P, 1], F32, tag="rstd")
-            nc.gpsimd.tensor_tensor(out=rstd[:], in0=var_eps[:], in1=minus_half[:], op=ALU.pow)
-            scale_pm[f] = small.tile([P, 2], F32, tag="scale_pm", name="scale_pm_%d" % f)
-            nc.gpsimd.tensor_scalar(
-                out=scale_pm[f][:], in0=gain_pm[:, f, :], scalar1=rstd[:], scalar2=1.0, op0=ALU.mult, op1=ALU.mult
+
+        def find_scale(f):
+            scale[f] = small.tile([P, 2], F32, tag="scale", name="scale_%d" % f)
+            nc.vector.tensor_scalar(
+                out=scale[f][:], in0=gain_pm[:, f, :], scalar1=rstd[f][:], scalar2=None, op0=ALU.mult
             )
+
+        def find_shift(f):
             shift[f] = small.tile([P, 1], F32, tag="shift", name="shift_%d" % f)
-            nc.gpsimd.tensor_scalar(
+            nc.vector.scalar_tensor_tensor(
                 out=shift[f][:],
-                in0=mean_var[:, 0:1],
-                scalar1=scale_pm[f][:, 1:2],
-                scalar2=beta[:, f : f + 1],
+                in0=mean_var[f][:, 0:1],
+                scalar=scale[f][:, 1:2],
+                in1=beta[:, f : f + 1],
                 op0=ALU.mult,
                 op1=ALU.add,
             )
@@ -214,20 +236,24 @@ def tile_attention_pb_kernel(tc, h_attn, proj_w, proj_g, proj_b, out):
         def norm(f):
             for half in range(HALVES):
                 z[(f, half)] = work.tile([P, BANK], F32, tag="z%d" % half, name="z_%d_%d" % (f, half))
-                nc.scalar.activation(
-                    out=z[(f, half)][:],
-                    in_=y[(f, half)][:],
-                    func=ACT.Identity,
-                    bias=shift[f][:],
-                    scale=scale_pm[f][:, 0:1],
-                )
+            nc.scalar.activation(
+                out=z[(f, 1)][:], in_=y[(f, 1)][:], func=ACT.Identity, bias=shift[f][:], scale=scale[f][:, 0:1]
+            )
+            (nc.gpsimd if Z_ENGINE == "gpsimd" else nc.vector).tensor_scalar(
+                out=z[(f, 0)][:],
+                in0=y_kept[f][:],
+                scalar1=scale[f][:, 0:1],
+                scalar2=shift[f][:],
+                op0=ALU.mult,
+                op1=ALU.add,
+            )
 
         zt = {}
 
         def transposes_back(f):
             for half in range(HALVES):
                 zt[(f, half)] = psum.tile(
-                    [P, BANK // P, P], F32, tag="bank%d" % (2 * IN_FLIGHT + half), name="zt_%d_%d" % (f, half)
+                    [P, BANK // P, P], F32, tag="bank%d" % (6 - 2 * (f % 2) + half), name="zt_%d_%d" % (f, half)
                 )
                 for j in range(JOBS):
                     for par in range(2):
@@ -237,44 +263,83 @@ def tile_attention_pb_kernel(tc, h_attn, proj_w, proj_g, proj_b, out):
         def store(f):
             for half in range(HALVES):
                 o = work.tile([P, BANK // P, P], F32, tag="o%d" % half)
-                if half == 0:
+                if half == 0 and f in X_ON_VECTOR:
                     nc.vector.tensor_copy(out=o[:], in_=zt[(f, half)][:])
                 else:
                     nc.scalar.copy(out=o[:], in_=zt[(f, half)][:])
                 nc.sync.dma_start(
-                    out=out_flat[half * BANK : (half + 1) * BANK, f * P : (f + 1) * P].rearrange(
-                        "(p m) c -> p m c", p=P
-                    ),
+                    out=out_flat[half * BANK : (half + 1) * BANK, f * P : (f + 1) * P].rearrange("(p m) c -> p m c", p=P),
                     in_=o[:],
                 )
 
-        for f in range(IN_FLIGHT - 1):
-            for half in range(HALVES):
-                products(f, half, [0, 1])
-        regroup_late_w(0)
-        for f in range(IN_FLIGHT - 1):
-            products(f, 0, [2])
-        regroup_late_w(1)
-        for f in range(IN_FLIGHT - 1):
-            products(f, 1, [2])
-        regroup_late_w(2)
-        for half in range(HALVES):
-            products(IN_FLIGHT - 1, half, list(range(PASSES)))
+        transpose_h(0)
+        for n in range(H_JOBS):
+            hard_swish(n)
+            if n >= 2 and n % 2 == 0:
+                quantise_h(*h_jobs[n - 1][:2])
+            for w_job in w_slots[n]:
+                regroup_w(*w_job)
+            if n == 3:
+                gb_bank = psum.tile([P, BANK], F32, tag="bank6")
+                nc.tensor.transpose(gb_bank[:, 0:P], gb_f32[:], ident[:])
+                gain_pm = keep.tile([P, FEAT_TILES, 2], F32)
+                nc.scalar.copy(out=gain_pm[:, :, 0], in_=gb_bank[:, 0:FEAT_TILES])
+                nc.scalar.mul(out=gain_pm[:, :, 1], in_=gb_bank[:, 0:FEAT_TILES], mul=-1.0)
+                beta = keep.tile([P, FEAT_TILES], F32)
+                nc.scalar.copy(out=beta[:], in_=gb_bank[:, FEAT_TILES : 2 * FEAT_TILES])
+            if n + 1 < H_JOBS:
+                transpose_h(n + 1)
+            if n >= 1:
+                for fh, g, j in w_slots[n - 1]:
+                    if j == JOBS - 1:
+                        quantise_w(fh, g)
+            for f in KEEP_AT.get(n, []):
+                keep_early(f)
+            for f in STATS_AT.get(n, []):
+                early_statistics(f)
+            for f in PRODUCTS_AT.get(n, []):
+                products(f, 0, [0, 1, 2], [6, 7, 4, 5][f % 4])
 
-        for f in range(IN_FLIGHT - 1):
-            statistics(f)
-            norm(f)
-        for g in range(PASSES):
-            nc.vector.quantize_mx(
-                out=w_codes[(g, 1)][:].bitcast(FP8X4), scales=w_scales[(g, 1)][:], in_=late_w_grouped[g][:]
-            )
-        for f in range(FEAT_TILES):
-            if f + IN_FLIGHT - 1 < FEAT_TILES:
-                statistics(f + IN_FLIGHT - 1)
-            transposes_back(f)
-            if f + IN_FLIGHT < FEAT_TILES:
-                for half in range(HALVES):
-                    products(f + IN_FLIGHT, half, list(range(PASSES)))
-            store(f)
-            if f + IN_FLIGHT - 1 < FEAT_TILES:
-                norm(f + IN_FLIGHT - 1)
+        for f in range(2):
+            products(f, 1, [0, 1], f)
+        quantise_h(HALVES - 1, PASSES - 1)
+        for f in range(2, IN_FLIGHT):
+            products(f, 1, [0, 1], f)
+        products(0, 1, [2], 0)
+        products(1, 1, [2], 1)
+        keep_early(5)
+        early_statistics(0)
+        late_stats(0)
+        aggregate(0)
+        products(6, 0, [0, 1, 2], 4)
+        products(2, 1, [2], 2)
+        products(3, 1, [2], 3)
+        products(7, 0, [0, 1, 2], 5)
+        keep_early(6)
+        early_statistics(1)
+        find_scale(0)
+        find_shift(0)
+        late_stats(1)
+        early_statistics(2)
+        aggregate(1)
+
+        for f in range(FEAT_TILES + 1):
+            if f < FEAT_TILES:
+                norm(f)
+                transposes_back(f)
+                if f + IN_FLIGHT < FEAT_TILES:
+                    products(f + IN_FLIGHT, 1, [0, 1, 2], f % IN_FLIGHT)
+            if f == 0:
+                keep_early(7)
+            if f > 0:
+                store(f - 1)
+            if f + 2 < FEAT_TILES:
+                late_stats(f + 2)
+            if f + 1 < FEAT_TILES:
+                find_scale(f + 1)
+            if f + 3 < FEAT_TILES:
+                early_statistics(f + 3)
+            if f + 1 < FEAT_TILES:
+                find_shift(f + 1)
+            if f + 2 < FEAT_TILES:
+                aggregate(f + 2)

@@ -28,10 +28,14 @@ LEAD = 2
 EPS = 1e-5
 W_BESIDE = [1, 2, 1, 2, 1, 2, 1, 2, 0, 0, 0, 0]
 W_ON_VECTOR = (2, 5)
-PRODUCTS_AT = {7: [0], 8: [1, 2], 9: [3], 10: [4], 11: [5]}
-KEEP_AT = {8: [0], 9: [1, 2], 10: [3], 11: [4]}
+PRODUCTS_AT = {7: [0], 8: [1, 2], 9: [3], 10: [4, 5], 11: [6, 7]}
+KEEP_AT = {8: [0], 9: [1, 2], 10: [3], 11: [4, 5], 12: [6, 7]}
+POOL_JOBS = ()
+POOL_PIECE = 256
+POOL_LOADS = (0, 3, 6)
+POOL_COPY_ON_VECTOR = ()
 STATS_AT = {}
-X_ON_VECTOR = (1, 4, 7)
+X_ON_VECTOR = (0, 2, 4, 5, 6, 7)
 Z_ENGINE = "gpsimd"
 SPLIT_FIRST = True
 
@@ -48,16 +52,19 @@ def tile_attention_pb_kernel(tc, h_attn, proj_w, proj_g, proj_b, out):
 
     with tc.tile_pool(name="keep", bufs=1) as keep, tc.tile_pool(name="work", bufs=3) as work, tc.tile_pool(
         name="small", bufs=4
-    ) as small, tc.psum_pool(name="psum", bufs=1) as psum, tc.manual_schedule():
+    ) as small, tc.tile_pool(name="result", bufs=5) as result, tc.psum_pool(name="psum", bufs=1) as psum, tc.manual_schedule():
         h_raw = {}
         w_raw = {}
 
         def load_h(half, g, j):
             h_raw[(half, g, j)] = keep.tile([P, JOB // P, K_PASS], BF16, name="h_raw_%d_%d_%d" % (half, g, j))
             rows = h_flat[half * BANK : (half + 1) * BANK, g * K_PASS : (g + 1) * K_PASS]
-            nc.sync.dma_start(
-                out=h_raw[(half, g, j)][:], in_=rows.rearrange("(i p j) k -> j p i k", p=P, j=JOBS)[j]
-            )
+            rows = rows.rearrange("(i p j) k -> j p i k", p=P, j=JOBS)[j]
+            if SPLIT_FIRST and (half, g, j) == h_jobs[0]:
+                for i in range(JOB // P):
+                    nc.sync.dma_start(out=h_raw[(half, g, j)][:, i, :], in_=rows[:, i, :])
+            else:
+                nc.sync.dma_start(out=h_raw[(half, g, j)][:], in_=rows)
 
         def load_w(fh, g, j):
             w_raw[(fh, g, j)] = keep.tile([P, JOB // P, K_PASS], BF16, name="w_raw_%d_%d_%d" % (fh, g, j))
@@ -73,9 +80,13 @@ def tile_attention_pb_kernel(tc, h_attn, proj_w, proj_g, proj_b, out):
         nc.scalar.dma_start(out=gb_rows[FEAT_TILES : 2 * FEAT_TILES, :], in_=proj_b.rearrange("(f p) -> f p", p=P))
 
         for n in range(H_JOBS):
-            load_h(*h_jobs[n])
+            if n not in POOL_JOBS:
+                load_h(*h_jobs[n])
             for w_job in w_slots[n]:
                 load_w(*w_job)
+            for i in range(len(POOL_JOBS)):
+                if n == POOL_LOADS[i]:
+                    load_h(*h_jobs[POOL_JOBS[i]])
 
         ident = keep.tile([P, P], F32)
         make_identity(nc, ident[:])
@@ -102,7 +113,45 @@ def tile_attention_pb_kernel(tc, h_attn, proj_w, proj_g, proj_b, out):
 
         h_banks = {}
 
+        h_ready = {}
+
+        def pool_hard_swish(n):
+            h_ready[n] = keep.tile([P, JOB // P, K_PASS], BF16, name="h_ready_%d" % n)
+            for i in range(JOB // P):
+                for k0 in range(0, K_PASS, POOL_PIECE):
+                    v = h_raw[h_jobs[n]][:, i, k0 : k0 + POOL_PIECE]
+                    line = work.tile([P, POOL_PIECE], F32, tag="line")
+                    nc.gpsimd.tensor_scalar(out=line[:], in0=v, scalar1=1.0 / 6.0, scalar2=0.5, op0=ALU.mult, op1=ALU.add)
+                    clamped = work.tile([P, POOL_PIECE], F32, tag="clamped")
+                    nc.gpsimd.tensor_scalar(out=clamped[:], in0=line[:], scalar1=0.0, scalar2=1.0, op0=ALU.max, op1=ALU.min)
+                    nc.gpsimd.tensor_tensor(
+                        out=h_ready[n][:, i, k0 : k0 + POOL_PIECE], in0=clamped[:], in1=v, op=ALU.mult
+                    )
+
+        def transpose_ready(n):
+            h_banks[n] = psum.tile([P, 2, JOB], F32, tag="bank%d" % (n % 4), name="h_bank_%d" % n)
+            for i in range(JOB // P):
+                words = h_ready[n][:, i, :].bitcast(F32)
+                for u in range(2):
+                    nc.tensor.transpose(h_banks[n][:, u, i * P : (i + 1) * P], words[:, u:WORDS:2], ident[:])
+
+        def copy_ready(n):
+            half, g, j = h_jobs[n]
+            if j == 0:
+                h_grouped[(half, g)] = work.tile(
+                    [P, 4 * BANK], BF16, align_bytes=64, tag="h_grouped", name="h_grouped_%d_%d" % (half, g)
+                )
+            (nc.vector.tensor_copy if n in POOL_COPY_ON_VECTOR else nc.scalar.copy)(
+                out=h_grouped[(half, g)][:, j * 4 * JOB : (j + 1) * 4 * JOB]
+                .bitcast(F32)
+                .rearrange("p (par x u) -> p par x u", par=2, u=2),
+                in_=h_banks[n][:].rearrange("p u (x par) -> p par x u", par=2),
+            )
+
         def transpose_h(n):
+            if n in POOL_JOBS:
+                transpose_ready(n)
+                return
             pieces = JOB // P if SPLIT_FIRST and n == 0 else 1
             h_banks[n] = []
             for piece in range(pieces):
@@ -119,6 +168,9 @@ def tile_attention_pb_kernel(tc, h_attn, proj_w, proj_g, proj_b, out):
         h_grouped = {}
 
         def hard_swish(n):
+            if n in POOL_JOBS:
+                copy_ready(n)
+                return
             half, g, j = h_jobs[n]
             if j == 0:
                 h_grouped[(half, g)] = work.tile(
@@ -209,6 +261,8 @@ def tile_attention_pb_kernel(tc, h_attn, proj_w, proj_g, proj_b, out):
         def aggregate(f):
             mean_var[f] = small.tile([P, 2], F32, tag="mean_var", name="mean_var_%d" % f)
             nc.vector.bn_aggr(out=mean_var[f][:], in_=stats[f][:].rearrange("p a s -> p (a s)"))
+
+        def find_rstd(f):
             rstd[f] = small.tile([P, 1], F32, tag="rstd", name="rstd_%d" % f)
             nc.scalar.activation(
                 out=rstd[f][:], in_=mean_var[f][:, 1:2], func=ACT.Abs_reciprocal_sqrt, bias=EPS, scale=1.0
@@ -251,7 +305,7 @@ def tile_attention_pb_kernel(tc, h_attn, proj_w, proj_g, proj_b, out):
         zt = {}
 
         def transposes_back(f):
-            for half in range(HALVES):
+            for half in (1, 0):
                 zt[(f, half)] = psum.tile(
                     [P, BANK // P, P], F32, tag="bank%d" % (6 - 2 * (f % 2) + half), name="zt_%d_%d" % (f, half)
                 )
@@ -261,8 +315,8 @@ def tile_attention_pb_kernel(tc, h_attn, proj_w, proj_g, proj_b, out):
                         nc.tensor.transpose(zt[(f, half)][:, 2 * par + j, :], z[(f, half)][:, i * P : (i + 1) * P], ident[:])
 
         def store(f):
-            for half in range(HALVES):
-                o = work.tile([P, BANK // P, P], F32, tag="o%d" % half)
+            for half in (1, 0):
+                o = result.tile([P, BANK // P, P], F32, tag="o%d" % half)
                 if half == 0 and f in X_ON_VECTOR:
                     nc.vector.tensor_copy(out=o[:], in_=zt[(f, half)][:])
                 else:
@@ -271,6 +325,9 @@ def tile_attention_pb_kernel(tc, h_attn, proj_w, proj_g, proj_b, out):
                     out=out_flat[half * BANK : (half + 1) * BANK, f * P : (f + 1) * P].rearrange("(p m) c -> p m c", p=P),
                     in_=o[:],
                 )
+
+        for n in POOL_JOBS:
+            pool_hard_swish(n)
 
         transpose_h(0)
         for n in range(H_JOBS):
@@ -300,22 +357,19 @@ def tile_attention_pb_kernel(tc, h_attn, proj_w, proj_g, proj_b, out):
             for f in PRODUCTS_AT.get(n, []):
                 products(f, 0, [0, 1, 2], [6, 7, 4, 5][f % 4])
 
-        for f in range(2):
+        for f in range(LEAD):
             products(f, 1, [0, 1], f)
         quantise_h(HALVES - 1, PASSES - 1)
-        for f in range(2, IN_FLIGHT):
-            products(f, 1, [0, 1], f)
-        products(0, 1, [2], 0)
-        products(1, 1, [2], 1)
-        keep_early(5)
+        for f in range(LEAD):
+            products(f, 1, [2], f)
+        for f in range(LEAD, IN_FLIGHT):
+            products(f, 1, [0, 1, 2], f)
+        for f in KEEP_AT[H_JOBS]:
+            keep_early(f)
         early_statistics(0)
         late_stats(0)
         aggregate(0)
-        products(6, 0, [0, 1, 2], 4)
-        products(2, 1, [2], 2)
-        products(3, 1, [2], 3)
-        products(7, 0, [0, 1, 2], 5)
-        keep_early(6)
+        find_rstd(0)
         early_statistics(1)
         find_scale(0)
         find_shift(0)
@@ -329,17 +383,17 @@ def tile_attention_pb_kernel(tc, h_attn, proj_w, proj_g, proj_b, out):
                 transposes_back(f)
                 if f + IN_FLIGHT < FEAT_TILES:
                     products(f + IN_FLIGHT, 1, [0, 1, 2], f % IN_FLIGHT)
-            if f == 0:
-                keep_early(7)
-            if f > 0:
-                store(f - 1)
+            if f + 1 < FEAT_TILES:
+                find_rstd(f + 1)
             if f + 2 < FEAT_TILES:
                 late_stats(f + 2)
             if f + 1 < FEAT_TILES:
                 find_scale(f + 1)
-            if f + 3 < FEAT_TILES:
-                early_statistics(f + 3)
-            if f + 1 < FEAT_TILES:
-                find_shift(f + 1)
             if f + 2 < FEAT_TILES:
                 aggregate(f + 2)
+            if f + 1 < FEAT_TILES:
+                find_shift(f + 1)
+            if f > 0:
+                store(f - 1)
+            if f + 3 < FEAT_TILES:
+                early_statistics(f + 3)

@@ -26,18 +26,16 @@ H_JOBS = STEPS * JOBS
 IN_FLIGHT = 4
 LEAD = 2
 EPS = 1e-5
-W_BESIDE = [1, 2, 1, 2, 1, 2, 1, 2, 0, 0, 0, 0]
-W_ON_VECTOR = (2, 5)
+W_BESIDE = [0, 2, 1, 2, 1, 2, 1, 2, 1, 0, 0, 0]
+W_ON_VECTOR = (1,)
 PRODUCTS_AT = {7: [0], 8: [1, 2], 9: [3], 10: [4, 5], 11: [6, 7]}
 KEEP_AT = {8: [0], 9: [1, 2], 10: [3], 11: [4, 5], 12: [6, 7]}
-POOL_JOBS = ()
-POOL_PIECE = 256
-POOL_LOADS = (0, 3, 6)
-POOL_COPY_ON_VECTOR = ()
-STATS_AT = {}
-X_ON_VECTOR = (0, 2, 4, 5, 6, 7)
+X_ON_VECTOR = (2, 4, 5, 6, 7)
 Z_ENGINE = "gpsimd"
 SPLIT_FIRST = True
+LAST_PIECES = 1
+R_FIRST = 1
+STATS_AT = {}
 
 FLOPS = 2 * ROWS * FEATS * K
 
@@ -80,13 +78,9 @@ def tile_attention_pb_kernel(tc, h_attn, proj_w, proj_g, proj_b, out):
         nc.scalar.dma_start(out=gb_rows[FEAT_TILES : 2 * FEAT_TILES, :], in_=proj_b.rearrange("(f p) -> f p", p=P))
 
         for n in range(H_JOBS):
-            if n not in POOL_JOBS:
-                load_h(*h_jobs[n])
+            load_h(*h_jobs[n])
             for w_job in w_slots[n]:
                 load_w(*w_job)
-            for i in range(len(POOL_JOBS)):
-                if n == POOL_LOADS[i]:
-                    load_h(*h_jobs[POOL_JOBS[i]])
 
         ident = keep.tile([P, P], F32)
         make_identity(nc, ident[:])
@@ -113,45 +107,7 @@ def tile_attention_pb_kernel(tc, h_attn, proj_w, proj_g, proj_b, out):
 
         h_banks = {}
 
-        h_ready = {}
-
-        def pool_hard_swish(n):
-            h_ready[n] = keep.tile([P, JOB // P, K_PASS], BF16, name="h_ready_%d" % n)
-            for i in range(JOB // P):
-                for k0 in range(0, K_PASS, POOL_PIECE):
-                    v = h_raw[h_jobs[n]][:, i, k0 : k0 + POOL_PIECE]
-                    line = work.tile([P, POOL_PIECE], F32, tag="line")
-                    nc.gpsimd.tensor_scalar(out=line[:], in0=v, scalar1=1.0 / 6.0, scalar2=0.5, op0=ALU.mult, op1=ALU.add)
-                    clamped = work.tile([P, POOL_PIECE], F32, tag="clamped")
-                    nc.gpsimd.tensor_scalar(out=clamped[:], in0=line[:], scalar1=0.0, scalar2=1.0, op0=ALU.max, op1=ALU.min)
-                    nc.gpsimd.tensor_tensor(
-                        out=h_ready[n][:, i, k0 : k0 + POOL_PIECE], in0=clamped[:], in1=v, op=ALU.mult
-                    )
-
-        def transpose_ready(n):
-            h_banks[n] = psum.tile([P, 2, JOB], F32, tag="bank%d" % (n % 4), name="h_bank_%d" % n)
-            for i in range(JOB // P):
-                words = h_ready[n][:, i, :].bitcast(F32)
-                for u in range(2):
-                    nc.tensor.transpose(h_banks[n][:, u, i * P : (i + 1) * P], words[:, u:WORDS:2], ident[:])
-
-        def copy_ready(n):
-            half, g, j = h_jobs[n]
-            if j == 0:
-                h_grouped[(half, g)] = work.tile(
-                    [P, 4 * BANK], BF16, align_bytes=64, tag="h_grouped", name="h_grouped_%d_%d" % (half, g)
-                )
-            (nc.vector.tensor_copy if n in POOL_COPY_ON_VECTOR else nc.scalar.copy)(
-                out=h_grouped[(half, g)][:, j * 4 * JOB : (j + 1) * 4 * JOB]
-                .bitcast(F32)
-                .rearrange("p (par x u) -> p par x u", par=2, u=2),
-                in_=h_banks[n][:].rearrange("p u (x par) -> p par x u", par=2),
-            )
-
         def transpose_h(n):
-            if n in POOL_JOBS:
-                transpose_ready(n)
-                return
             pieces = JOB // P if SPLIT_FIRST and n == 0 else 1
             h_banks[n] = []
             for piece in range(pieces):
@@ -168,9 +124,6 @@ def tile_attention_pb_kernel(tc, h_attn, proj_w, proj_g, proj_b, out):
         h_grouped = {}
 
         def hard_swish(n):
-            if n in POOL_JOBS:
-                copy_ready(n)
-                return
             half, g, j = h_jobs[n]
             if j == 0:
                 h_grouped[(half, g)] = work.tile(
@@ -246,6 +199,8 @@ def tile_attention_pb_kernel(tc, h_attn, proj_w, proj_g, proj_b, out):
             nc.scalar.copy(out=y_kept[f][:], in_=y[(f, 0)][:])
 
         def early_statistics(f):
+            if f in stats:
+                return
             stats[f] = keep.tile([P, HALVES, 6], F32, name="stats_%d" % f)
             nc.vector.bn_stats(out=stats[f][:, 0, :], in_=y_kept[f][:])
 
@@ -293,7 +248,7 @@ def tile_attention_pb_kernel(tc, h_attn, proj_w, proj_g, proj_b, out):
             nc.scalar.activation(
                 out=z[(f, 1)][:], in_=y[(f, 1)][:], func=ACT.Identity, bias=shift[f][:], scale=scale[f][:, 0:1]
             )
-            (nc.gpsimd if Z_ENGINE == "gpsimd" else nc.vector).tensor_scalar(
+            nc.gpsimd.tensor_scalar(
                 out=z[(f, 0)][:],
                 in0=y_kept[f][:],
                 scalar1=scale[f][:, 0:1],
@@ -316,18 +271,17 @@ def tile_attention_pb_kernel(tc, h_attn, proj_w, proj_g, proj_b, out):
 
         def store(f):
             for half in (1, 0):
-                o = result.tile([P, BANK // P, P], F32, tag="o%d" % half)
-                if half == 0 and f in X_ON_VECTOR:
-                    nc.vector.tensor_copy(out=o[:], in_=zt[(f, half)][:])
-                else:
-                    nc.scalar.copy(out=o[:], in_=zt[(f, half)][:])
-                nc.sync.dma_start(
-                    out=out_flat[half * BANK : (half + 1) * BANK, f * P : (f + 1) * P].rearrange("(p m) c -> p m c", p=P),
-                    in_=o[:],
-                )
-
-        for n in POOL_JOBS:
-            pool_hard_swish(n)
+                on_vector = half == 0 and f in X_ON_VECTOR
+                rows = out_flat[half * BANK : (half + 1) * BANK, f * P : (f + 1) * P].rearrange("(p m) c -> p m c", p=P)
+                pieces = LAST_PIECES if f == FEAT_TILES - 1 else 1
+                step = BANK // P // pieces
+                for m in range(0, BANK // P, step):
+                    o = result.tile([P, step, P], F32, tag="o%d%d" % (half, pieces), name="o_%d_%d_%d" % (f, half, m))
+                    if on_vector:
+                        nc.vector.tensor_copy(out=o[:], in_=zt[(f, half)][:, m : m + step, :])
+                    else:
+                        nc.scalar.copy(out=o[:], in_=zt[(f, half)][:, m : m + step, :])
+                    nc.sync.dma_start(out=rows[:, m : m + step, :], in_=o[:])
 
         transpose_h(0)
         for n in range(H_JOBS):
@@ -339,11 +293,19 @@ def tile_attention_pb_kernel(tc, h_attn, proj_w, proj_g, proj_b, out):
             if n == 3:
                 gb_bank = psum.tile([P, BANK], F32, tag="bank6")
                 nc.tensor.transpose(gb_bank[:, 0:P], gb_f32[:], ident[:])
+                gain_beta = keep.tile([P, 2 * FEAT_TILES], F32)
+                nc.scalar.copy(out=gain_beta[:], in_=gb_bank[:, 0 : 2 * FEAT_TILES])
+                beta = gain_beta[:, FEAT_TILES : 2 * FEAT_TILES]
                 gain_pm = keep.tile([P, FEAT_TILES, 2], F32)
-                nc.scalar.copy(out=gain_pm[:, :, 0], in_=gb_bank[:, 0:FEAT_TILES])
-                nc.scalar.mul(out=gain_pm[:, :, 1], in_=gb_bank[:, 0:FEAT_TILES], mul=-1.0)
-                beta = keep.tile([P, FEAT_TILES], F32)
-                nc.scalar.copy(out=beta[:], in_=gb_bank[:, FEAT_TILES : 2 * FEAT_TILES])
+                for i, sign in enumerate((1.0, -1.0)):
+                    nc.gpsimd.tensor_scalar(
+                        out=gain_pm[:, :, i],
+                        in0=gain_beta[:, 0:FEAT_TILES],
+                        scalar1=sign,
+                        scalar2=0.0,
+                        op0=ALU.mult,
+                        op1=ALU.add,
+                    )
             if n + 1 < H_JOBS:
                 transpose_h(n + 1)
             if n >= 1:
@@ -378,12 +340,14 @@ def tile_attention_pb_kernel(tc, h_attn, proj_w, proj_g, proj_b, out):
         aggregate(1)
 
         for f in range(FEAT_TILES + 1):
+            if R_FIRST <= f and f + 1 < FEAT_TILES:
+                find_rstd(f + 1)
             if f < FEAT_TILES:
                 norm(f)
                 transposes_back(f)
                 if f + IN_FLIGHT < FEAT_TILES:
                     products(f + IN_FLIGHT, 1, [0, 1, 2], f % IN_FLIGHT)
-            if f + 1 < FEAT_TILES:
+            if f < R_FIRST and f + 1 < FEAT_TILES:
                 find_rstd(f + 1)
             if f + 2 < FEAT_TILES:
                 late_stats(f + 2)

@@ -57,7 +57,7 @@ def tile_attention_pb_kernel(tc, h_attn, proj_w, proj_g, proj_b, out):
         def load_h(half, g, j):
             h_raw[(half, g, j)] = keep.tile([P, JOB // P, K_PASS], BF16, name="h_raw_%d_%d_%d" % (half, g, j))
             rows = h_flat[half * BANK : (half + 1) * BANK, g * K_PASS : (g + 1) * K_PASS]
-            rows = rows.rearrange("(i p j) k -> j p i k", p=P, j=JOBS)[j]
+            rows = rows.rearrange("(p i j) k -> j p i k", p=P, j=JOBS)[j]
             if SPLIT_FIRST and (half, g, j) == h_jobs[0]:
                 for i in range(JOB // P):
                     nc.sync.dma_start(out=h_raw[(half, g, j)][:, i, :], in_=rows[:, i, :])
@@ -117,9 +117,10 @@ def tile_attention_pb_kernel(tc, h_attn, proj_w, proj_g, proj_b, out):
                 h_banks[n].append(bank)
                 for i in range(JOB // P // pieces):
                     words = h_raw[h_jobs[n]][:, piece + i, :].bitcast(F32)
-                    part = bank[:, i * 2 * P : (i + 1) * 2 * P].rearrange("p (m u par) -> p u m par", u=2, par=2)
                     for u in range(2):
-                        nc.tensor.transpose(part[:, u, :, :], words[:, u:WORDS:2], ident[:])
+                        nc.tensor.transpose(
+                            bank[:, i * 2 * P + u : (i + 1) * 2 * P : 2], words[:, u:WORDS:2], ident[:]
+                        )
 
         h_grouped = {}
 
@@ -130,21 +131,20 @@ def tile_attention_pb_kernel(tc, h_attn, proj_w, proj_g, proj_b, out):
                     [P, 4 * BANK], BF16, align_bytes=64, tag="h_grouped", name="h_grouped_%d_%d" % (half, g)
                 )
             pieces = len(h_banks[n])
+            cols = 4 * JOB // pieces
             for piece in range(pieces):
-                ramp = work.tile([P, 2, JOB // pieces, 2], F32, tag="ramp")
-                v = h_banks[n][piece][:].bitcast(BF16).rearrange("p (y par e) -> p par y e", par=2, e=2)
-                ys = slice(piece * JOB // pieces, (piece + 1) * JOB // pieces)
+                v = h_banks[n][piece][:].bitcast(BF16)
+                ramp = work.tile([P, cols], F32, tag="ramp")
                 nc.scalar.activation(out=ramp[:], in_=v, func=ACT.Relu, bias=0.5, scale=1.0 / 6.0)
-                for par in range(2):
-                    cols = h_grouped[(half, g)][:, (2 * j + par) * 2 * JOB : (2 * j + par + 1) * 2 * JOB]
-                    nc.vector.scalar_tensor_tensor(
-                        out=cols.rearrange("p (y e) -> p y e", e=2)[:, ys, :],
-                        in0=ramp[:, par, :, :],
-                        scalar=1.0,
-                        in1=v[:, par, :, :],
-                        op0=ALU.min,
-                        op1=ALU.mult,
-                    )
+                col0 = j * 4 * JOB + piece * cols
+                nc.vector.scalar_tensor_tensor(
+                    out=h_grouped[(half, g)][:, col0 : col0 + cols],
+                    in0=ramp[:],
+                    scalar=1.0,
+                    in1=v,
+                    op0=ALU.min,
+                    op1=ALU.mult,
+                )
 
         def quantise_h(half, g):
             nc.vector.quantize_mx(
@@ -265,9 +265,9 @@ def tile_attention_pb_kernel(tc, h_attn, proj_w, proj_g, proj_b, out):
                     [P, BANK // P, P], F32, tag="bank%d" % (6 - 2 * (f % 2) + half), name="zt_%d_%d" % (f, half)
                 )
                 for j in range(JOBS):
-                    for par in range(2):
-                        i = 2 * j + par
-                        nc.tensor.transpose(zt[(f, half)][:, 2 * par + j, :], z[(f, half)][:, i * P : (i + 1) * P], ident[:])
+                    for i in range(JOB // P):
+                        col0 = j * JOB + i * P
+                        nc.tensor.transpose(zt[(f, half)][:, 2 * i + j, :], z[(f, half)][:, col0 : col0 + P], ident[:])
 
         def store(f):
             for half in (1, 0):

@@ -24,12 +24,12 @@ JOBS = BANK // JOB
 STEPS = HALVES * PASSES
 H_JOBS = STEPS * JOBS
 IN_FLIGHT = 4
-LEAD = 2
+LEAD = 1
 EPS = 1e-5
 W_BESIDE = [0, 2, 1, 2, 1, 2, 1, 2, 1, 0, 0, 0]
-W_ON_VECTOR = (1,)
-PRODUCTS_AT = {7: [0], 8: [1, 2], 9: [3], 10: [4, 5], 11: [6, 7]}
-KEEP_AT = {8: [0], 9: [1, 2], 10: [3], 11: [4, 5], 12: [6, 7]}
+W_ON_VECTOR = (1, 4)
+PRODUCTS_AT = {7: [0], 8: [1], 9: [2], 10: [3, 4], 11: [5, 6, 7]}
+KEEP_AT = {8: [0], 9: [1], 10: [2], 11: [3, 4], 12: [5, 6, 7]}
 X_ON_VECTOR = (2, 4, 5, 6, 7)
 Z_ENGINE = "gpsimd"
 SPLIT_FIRST = True
@@ -149,6 +149,14 @@ def tile_attention_pb_kernel(tc, h_attn, proj_w, proj_g, proj_b, out):
         def quantise_h(half, g):
             nc.vector.quantize_mx(
                 out=h_codes[(half, g)][:].bitcast(FP8X4), scales=h_scales[(half, g)][:], in_=h_grouped[(half, g)][:]
+            )
+
+        def quantise_part(half, g, j):
+            rows = slice(j * JOB, (j + 1) * JOB)
+            nc.vector.quantize_mx(
+                out=h_codes[(half, g)][:, rows].bitcast(FP8X4),
+                scales=h_scales[(half, g)][:, rows],
+                in_=h_grouped[(half, g)][:, j * 4 * JOB : (j + 1) * 4 * JOB],
             )
 
         w_grouped = {}
@@ -321,7 +329,8 @@ def tile_attention_pb_kernel(tc, h_attn, proj_w, proj_g, proj_b, out):
 
         for f in range(LEAD):
             products(f, 1, [0, 1], f)
-        quantise_h(HALVES - 1, PASSES - 1)
+        for j in range(JOBS):
+            quantise_part(HALVES - 1, PASSES - 1, j)
         for f in range(LEAD):
             products(f, 1, [2], f)
         for f in range(LEAD, IN_FLIGHT):

import concourse.mybir as mybir
from concourse.masks import make_identity

F32 = mybir.dt.float32
BF16 = mybir.dt.bfloat16
U32 = mybir.dt.uint32
U8 = mybir.dt.uint8
FP8X4 = mybir.dt.float8_e4m3fn_x4
ACT = mybir.ActivationFunctionType
ALU = mybir.AluOpType

P = 128
ROWS = 1024
FEATS = 1024
K = 1536
K_PASS = 512
WORDS = K_PASS // 2
PASSES = K // K_PASS
BANK = 512
HALVES = 2
FEAT_TILES = FEATS // P
JOB = 256
JOBS = BANK // JOB
STEPS = HALVES * PASSES
H_JOBS = STEPS * JOBS
IN_FLIGHT = 4
LEAD = 1
EPS = 1e-5
W_BESIDE = [0, 2, 1, 2, 1, 2, 1, 2, 1, 0, 0, 0]
W_ON_VECTOR = (1, 4)
PRODUCTS_AT = {7: [0], 8: [1], 9: [2], 10: [3, 4], 11: [5, 6, 7]}
KEEP_AT = {8: [0], 9: [1], 10: [2], 11: [3, 4], 12: [5, 6, 7]}
X_ON_VECTOR = (2, 4, 5, 6, 7)
Z_ENGINE = "gpsimd"
SPLIT_FIRST = True
LAST_PIECES = 1
R_FIRST = 1
STATS_AT = {}

FLOPS = 2 * ROWS * FEATS * K


def tile_attention_pb_kernel(tc, h_attn, proj_w, proj_g, proj_b, out):
    nc = tc.nc
    h_flat = h_attn.flatten_outer_dims()
    out_flat = out.flatten_outer_dims()
    h_jobs = [(half, g, j) for half in range(HALVES) for g in range(PASSES) for j in range(JOBS)]
    w_jobs = [(fh, g, j) for fh in range(HALVES) for g in range(PASSES) for j in range(JOBS)]
    w_slots = [w_jobs[sum(W_BESIDE[:n]) : sum(W_BESIDE[: n + 1])] for n in range(H_JOBS)]

    with tc.tile_pool(name="keep", bufs=1) as keep, tc.tile_pool(name="work", bufs=3) as work, tc.tile_pool(
        name="small", bufs=4
    ) as small, tc.tile_pool(name="result", bufs=5) as result, tc.psum_pool(name="psum", bufs=1) as psum, tc.manual_schedule():
        h_raw = {}
        w_raw = {}

        def load_h(half, g, j):
            h_raw[(half, g, j)] = keep.tile([P, JOB // P, K_PASS], BF16, name="h_raw_%d_%d_%d" % (half, g, j))
            rows = h_flat[half * BANK : (half + 1) * BANK, g * K_PASS : (g + 1) * K_PASS]
            rows = rows.rearrange("(p i j) k -> j p i k", p=P, j=JOBS)[j]
            if SPLIT_FIRST and (half, g, j) == h_jobs[0]:
                for i in range(JOB // P):
                    nc.sync.dma_start(out=h_raw[(half, g, j)][:, i, :], in_=rows[:, i, :])
            else:
                nc.sync.dma_start(out=h_raw[(half, g, j)][:], in_=rows)

        def load_w(fh, g, j):
            w_raw[(fh, g, j)] = keep.tile([P, JOB // P, K_PASS], BF16, name="w_raw_%d_%d_%d" % (fh, g, j))
            feat0 = fh * BANK + j * JOB
            nc.sync.dma_start(
                out=w_raw[(fh, g, j)][:],
                in_=proj_w[feat0 : feat0 + JOB, g * K_PASS : (g + 1) * K_PASS].rearrange("(i p) k -> p i k", p=P),
            )

        gb_rows = keep.tile([P, P], BF16)
        nc.vector.memset(gb_rows[:], 0.0)
        nc.scalar.dma_start(out=gb_rows[0:FEAT_TILES, :], in_=proj_g.rearrange("(f p) -> f p", p=P))
        nc.scalar.dma_start(out=gb_rows[FEAT_TILES : 2 * FEAT_TILES, :], in_=proj_b.rearrange("(f p) -> f p", p=P))

        for n in range(H_JOBS):
            load_h(*h_jobs[n])
            for w_job in w_slots[n]:
                load_w(*w_job)

        ident = keep.tile([P, P], F32)
        make_identity(nc, ident[:])

        one = keep.tile([P, 1], F32)
        nc.vector.memset(one[:], 1.0)
        warm = keep.tile([P, 1], F32)
        nc.scalar.activation(out=warm[:], in_=one[:], func=ACT.Abs_reciprocal_sqrt)

        gb_f32 = keep.tile([P, P], F32)
        nc.gpsimd.tensor_copy(out=gb_f32[:], in_=gb_rows[:])

        h_codes = {}
        h_scales = {}
        w_codes = {}
        w_scales = {}
        for half in range(HALVES):
            for g in range(PASSES):
                key = (half, g)
                h_codes[key] = keep.tile([P, BANK], U32, align_bytes=64, name="h_codes_%d_%d" % key)
                h_scales[key] = keep.tile([P, BANK], U8, align_bytes=64, name="h_scales_%d_%d" % key)
                w_codes[key] = keep.tile([P, BANK], U32, align_bytes=64, name="w_codes_%d_%d" % key)
                w_scales[key] = keep.tile([P, BANK], U8, align_bytes=64, name="w_scales_%d_%d" % key)

        h_banks = {}

        def transpose_h(n):
            pieces = JOB // P if SPLIT_FIRST and n == 0 else 1
            h_banks[n] = []
            for piece in range(pieces):
                bank = psum.tile(
                    [P, 2 * JOB // pieces], F32, tag="bank%d" % ((n + 3 * piece) % 4), name="h_bank_%d_%d" % (n, piece)
                )
                h_banks[n].append(bank)
                for i in range(JOB // P // pieces):
                    words = h_raw[h_jobs[n]][:, piece + i, :].bitcast(F32)
                    for u in range(2):
                        nc.tensor.transpose(
                            bank[:, i * 2 * P + u : (i + 1) * 2 * P : 2], words[:, u:WORDS:2], ident[:]
                        )

        h_grouped = {}

        def hard_swish(n):
            half, g, j = h_jobs[n]
            if j == 0:
                h_grouped[(half, g)] = work.tile(
                    [P, 4 * BANK], BF16, align_bytes=64, tag="h_grouped", name="h_grouped_%d_%d" % (half, g)
                )
            pieces = len(h_banks[n])
            cols = 4 * JOB // pieces
            for piece in range(pieces):
                v = h_banks[n][piece][:].bitcast(BF16)
                ramp = work.tile([P, cols], F32, tag="ramp")
                nc.scalar.activation(out=ramp[:], in_=v, func=ACT.Relu, bias=0.5, scale=1.0 / 6.0)
                col0 = j * 4 * JOB + piece * cols
                nc.vector.scalar_tensor_tensor(
                    out=h_grouped[(half, g)][:, col0 : col0 + cols],
                    in0=ramp[:],
                    scalar=1.0,
                    in1=v,
                    op0=ALU.min,
                    op1=ALU.mult,
                )

        def quantise_h(half, g):
            nc.vector.quantize_mx(
                out=h_codes[(half, g)][:].bitcast(FP8X4), scales=h_scales[(half, g)][:], in_=h_grouped[(half, g)][:]
            )

        def quantise_part(half, g, j):
            rows = slice(j * JOB, (j + 1) * JOB)
            nc.vector.quantize_mx(
                out=h_codes[(half, g)][:, rows].bitcast(FP8X4),
                scales=h_scales[(half, g)][:, rows],
                in_=h_grouped[(half, g)][:, j * 4 * JOB : (j + 1) * 4 * JOB],
            )

        w_grouped = {}

        def regroup_w(fh, g, j):
            if j == 0:
                w_grouped[(fh, g)] = work.tile(
                    [P, 4 * BANK], BF16, align_bytes=64, tag="w_grouped", name="w_grouped_%d_%d" % (fh, g)
                )
            w_bank = psum.tile([P, 2, JOB], F32, tag="bank%d" % (4 + j))
            for i in range(JOB // P):
                words = w_raw[(fh, g, j)][:, i, :].bitcast(F32)
                for u in range(2):
                    nc.tensor.transpose(w_bank[:, u, i * P : (i + 1) * P], words[:, u:WORDS:2], ident[:])
            (nc.vector.tensor_copy if w_jobs.index((fh, g, j)) in W_ON_VECTOR else nc.scalar.copy)(
                out=w_grouped[(fh, g)][:, j * 4 * JOB : (j + 1) * 4 * JOB].bitcast(F32).rearrange("p (c u) -> p c u", u=2),
                in_=w_bank[:].rearrange("p u c -> p c u"),
            )

        def quantise_w(fh, g):
            nc.vector.quantize_mx(
                out=w_codes[(fh, g)][:].bitcast(FP8X4), scales=w_scales[(fh, g)][:], in_=w_grouped[(fh, g)][:]
            )

        y = {}

        def products(f, half, passes, bank):
            fh = f // (BANK // P)
            feats = slice((f % (BANK // P)) * P, (f % (BANK // P) + 1) * P)
            if passes[0] == 0:
                y[(f, half)] = psum.tile([P, BANK], F32, tag="bank%d" % bank, name="y_%d_%d" % (f, half))
            for g in passes:
                nc.tensor.matmul_mx(
                    out=y[(f, half)][:],
                    lhsT=w_codes[(fh, g)][:, feats].bitcast(FP8X4),
                    lhsT_scale=w_scales[(fh, g)][:, feats],
                    rhs=h_codes[(half, g)][:].bitcast(FP8X4),
                    rhs_scale=h_scales[(half, g)][:],
                    start=(g == 0),
                    stop=(g == PASSES - 1),
                )

        y_kept = {}
        stats = {}

        def keep_early(f):
            y_kept[f] = keep.tile([P, BANK], F32, name="y_kept_%d" % f)
            nc.scalar.copy(out=y_kept[f][:], in_=y[(f, 0)][:])

        def early_statistics(f):
            if f in stats:
                return
            stats[f] = keep.tile([P, HALVES, 6], F32, name="stats_%d" % f)
            nc.vector.bn_stats(out=stats[f][:, 0, :], in_=y_kept[f][:])

        scale = {}
        shift = {}

        def late_stats(f):
            nc.vector.bn_stats(out=stats[f][:, 1, :], in_=y[(f, 1)][:])

        mean_var = {}
        rstd = {}

        def aggregate(f):
            mean_var[f] = small.tile([P, 2], F32, tag="mean_var", name="mean_var_%d" % f)
            nc.vector.bn_aggr(out=mean_var[f][:], in_=stats[f][:].rearrange("p a s -> p (a s)"))

        def find_rstd(f):
            rstd[f] = small.tile([P, 1], F32, tag="rstd", name="rstd_%d" % f)
            nc.scalar.activation(
                out=rstd[f][:], in_=mean_var[f][:, 1:2], func=ACT.Abs_reciprocal_sqrt, bias=EPS, scale=1.0
            )

        def find_scale(f):
            scale[f] = small.tile([P, 2], F32, tag="scale", name="scale_%d" % f)
            nc.vector.tensor_scalar(
                out=scale[f][:], in0=gain_pm[:, f, :], scalar1=rstd[f][:], scalar2=None, op0=ALU.mult
            )

        def find_shift(f):
            shift[f] = small.tile([P, 1], F32, tag="shift", name="shift_%d" % f)
            nc.vector.scalar_tensor_tensor(
                out=shift[f][:],
                in0=mean_var[f][:, 0:1],
                scalar=scale[f][:, 1:2],
                in1=beta[:, f : f + 1],
                op0=ALU.mult,
                op1=ALU.add,
            )

        z = {}

        def norm(f):
            for half in range(HALVES):
                z[(f, half)] = work.tile([P, BANK], F32, tag="z%d" % half, name="z_%d_%d" % (f, half))
            nc.scalar.activation(
                out=z[(f, 1)][:], in_=y[(f, 1)][:], func=ACT.Identity, bias=shift[f][:], scale=scale[f][:, 0:1]
            )
            nc.gpsimd.tensor_scalar(
                out=z[(f, 0)][:],
                in0=y_kept[f][:],
                scalar1=scale[f][:, 0:1],
                scalar2=shift[f][:],
                op0=ALU.mult,
                op1=ALU.add,
            )

        zt = {}

        def transposes_back(f):
            for half in (1, 0):
                zt[(f, half)] = psum.tile(
                    [P, BANK // P, P], F32, tag="bank%d" % (6 - 2 * (f % 2) + half), name="zt_%d_%d" % (f, half)
                )
                for j in range(JOBS):
                    for i in range(JOB // P):
                        col0 = j * JOB + i * P
                        nc.tensor.transpose(zt[(f, half)][:, 2 * i + j, :], z[(f, half)][:, col0 : col0 + P], ident[:])

        def store(f):
            for half in (1, 0):
                on_vector = half == 0 and f in X_ON_VECTOR
                rows = out_flat[half * BANK : (half + 1) * BANK, f * P : (f + 1) * P].rearrange("(p m) c -> p m c", p=P)
                pieces = LAST_PIECES if f == FEAT_TILES - 1 else 1
                step = BANK // P // pieces
                for m in range(0, BANK // P, step):
                    o = result.tile([P, step, P], F32, tag="o%d%d" % (half, pieces), name="o_%d_%d_%d" % (f, half, m))
                    if on_vector:
                        nc.vector.tensor_copy(out=o[:], in_=zt[(f, half)][:, m : m + step, :])
                    else:
                        nc.scalar.copy(out=o[:], in_=zt[(f, half)][:, m : m + step, :])
                    nc.sync.dma_start(out=rows[:, m : m + step, :], in_=o[:])

        transpose_h(0)
        for n in range(H_JOBS):
            hard_swish(n)
            if n >= 2 and n % 2 == 0:
                quantise_h(*h_jobs[n - 1][:2])
            for w_job in w_slots[n]:
                regroup_w(*w_job)
            if n == 3:
                gb_bank = psum.tile([P, BANK], F32, tag="bank6")
                nc.tensor.transpose(gb_bank[:, 0:P], gb_f32[:], ident[:])
                gain_beta = keep.tile([P, 2 * FEAT_TILES], F32)
                nc.scalar.copy(out=gain_beta[:], in_=gb_bank[:, 0 : 2 * FEAT_TILES])
                beta = gain_beta[:, FEAT_TILES : 2 * FEAT_TILES]
                gain_pm = keep.tile([P, FEAT_TILES, 2], F32)
                for i, sign in enumerate((1.0, -1.0)):
                    nc.gpsimd.tensor_scalar(
                        out=gain_pm[:, :, i],
                        in0=gain_beta[:, 0:FEAT_TILES],
                        scalar1=sign,
                        scalar2=0.0,
                        op0=ALU.mult,
                        op1=ALU.add,
                    )
            if n + 1 < H_JOBS:
                transpose_h(n + 1)
            if n >= 1:
                for fh, g, j in w_slots[n - 1]:
                    if j == JOBS - 1:
                        quantise_w(fh, g)
            for f in KEEP_AT.get(n, []):
                keep_early(f)
            for f in STATS_AT.get(n, []):
                early_statistics(f)
            for f in PRODUCTS_AT.get(n, []):
                products(f, 0, [0, 1, 2], [6, 7, 4, 5][f % 4])

        for f in range(LEAD):
            products(f, 1, [0, 1], f)
        for j in range(JOBS):
            quantise_part(HALVES - 1, PASSES - 1, j)
        for f in range(LEAD):
            products(f, 1, [2], f)
        for f in range(LEAD, IN_FLIGHT):
            products(f, 1, [0, 1, 2], f)
        for f in KEEP_AT[H_JOBS]:
            keep_early(f)
        early_statistics(0)
        late_stats(0)
        aggregate(0)
        find_rstd(0)
        early_statistics(1)
        find_scale(0)
        find_shift(0)
        late_stats(1)
        early_statistics(2)
        aggregate(1)

        for f in range(FEAT_TILES + 1):
            if R_FIRST <= f and f + 1 < FEAT_TILES:
                find_rstd(f + 1)
            if f < FEAT_TILES:
                norm(f)
                transposes_back(f)
                if f + IN_FLIGHT < FEAT_TILES:
                    products(f + IN_FLIGHT, 1, [0, 1, 2], f % IN_FLIGHT)
            if f < R_FIRST and f + 1 < FEAT_TILES:
                find_rstd(f + 1)
            if f + 2 < FEAT_TILES:
                late_stats(f + 2)
            if f + 1 < FEAT_TILES:
                find_scale(f + 1)
            if f + 2 < FEAT_TILES:
                aggregate(f + 2)
            if f + 1 < FEAT_TILES:
                find_shift(f + 1)
            if f > 0:
                store(f - 1)
            if f + 3 < FEAT_TILES:
                early_statistics(f + 3)
